import numpy as np
import ml_dtypes


def mxq(x, axis, fmt="e4m3"):
    dtype, down = {"e4m3": (ml_dtypes.float8_e4m3fn, 7), "e5m2": (ml_dtypes.float8_e5m2, 14)}[fmt]
    v = np.moveaxis(np.asarray(x, np.float32).astype(ml_dtypes.bfloat16).astype(np.float64), axis, -1)
    blocks = v.reshape(v.shape[:-1] + (-1, 32))
    amax = np.abs(blocks).max(-1, keepdims=True)
    byte = np.maximum(np.where(amax > 0, np.frexp(amax)[1] - 1 + 127, 0) - down, 1)
    scale = np.exp2(byte - 127.0)
    codes = (blocks / scale).astype(np.float32).astype(dtype).astype(np.float64)
    return np.moveaxis((codes * scale).reshape(v.shape), -1, axis)


WIDE = False


def mx_kscale(k):
    if not WIDE:
        return np.ones(k)
    levels = np.array([10, -10, 5, -5, 0])
    a = np.random.permutation(np.resize(levels, k // 512 * 4)).reshape(k // 512, 4)
    idx = np.arange(k)
    return np.exp2(a[idx // 512, idx % 128 // 32])


BF16 = ml_dtypes.bfloat16


def bf(x):
    return np.asarray(x, np.float32).astype(BF16)


def f64(x):
    return np.asarray(x).astype(np.float64)


E2M1 = np.array([0.0, 0.5, 1.0, 1.5, 2.0, 3.0, 4.0, 6.0, -0.0, -0.5, -1.0, -1.5, -2.0, -3.0, -4.0, -6.0])


def pack_weight(w, fmt):
    k, n = w.shape
    w = f64(bf(w)).reshape(k // 32, 32, n)
    amax = np.abs(w).max(1)
    if fmt == "e4m3":
        byte = np.frexp(amax)[1] - 1 + 127 - 7
    else:
        mant, ex = np.frexp(amax / 6.0)
        byte = np.where(mant > 0.5, ex, ex - 1) + 127
    byte = np.clip(np.where(amax > 0, byte, 1), 1, 254)
    scaled = (w * np.exp2(127.0 - byte)[:, None, :]).reshape(k, n).astype(np.float32)
    by_word = np.ascontiguousarray(scaled.reshape(k // 512, 128, 4, n).transpose(0, 1, 3, 2))
    if fmt == "e4m3":
        words = by_word.astype(ml_dtypes.float8_e4m3fn).view(np.uint8)
    else:
        c = by_word.astype(ml_dtypes.float4_e2m1fn).view(np.uint8) & 0xF
        words = c[..., 0::2] | (c[..., 1::2] << 4)
    return np.ascontiguousarray(words), np.ascontiguousarray(byte.astype(np.uint8).reshape(k // 512, 16, n))


def unpack_weight(words, scales, fmt):
    g, p, n, _ = words.shape
    if fmt == "e4m3":
        vals = np.ascontiguousarray(words).view(ml_dtypes.float8_e4m3fn).astype(np.float64)
    else:
        nib = np.empty((g, p, n, 4), np.uint8)
        nib[..., 0::2] = words & 0xF
        nib[..., 1::2] = words >> 4
        vals = E2M1[nib]
    vals = vals * np.repeat(np.exp2(scales.astype(np.float64) - 127.0), 8, axis=1)[..., None]
    return vals.transpose(0, 1, 3, 2).reshape(g * 512, n)


B, IN_DIM, MEM = 8192, 256, 256
DIN = MEM + IN_DIM
F = 2 * MEM
LN_EPS = 1e-5
FMT = "e4m3"


def erf(v):
    a = np.minimum(np.abs(v), 6.0)
    a2 = 2.0 * a * a
    term = a.copy()
    tot = a.copy()
    for n in range(1, 120):
        term = term * a2 / (2 * n + 1)
        tot = tot + term
    return np.sign(v) * (2.0 / np.sqrt(np.pi)) * np.exp(-a * a) * tot


def gelu_erf(v):
    return 0.5 * v * (1.0 + erf(v / np.sqrt(2.0)))


def layernorm(t, g, b):
    mu = t.mean(-1, keepdims=True)
    var = np.square(t - mu).mean(-1, keepdims=True)
    return (t - mu) / np.sqrt(var + LN_EPS) * g + b


def setup_inputs():
    s = mx_kscale(DIN)
    x = bf(np.random.standard_normal((B, IN_DIM)) * s[MEM:])
    h = bf(np.random.standard_normal((B, MEM)) * s[:MEM])
    W1_words, W1_scales = pack_weight(np.random.standard_normal((DIN, F)) * 1.3 / np.sqrt(DIN) / s[:, None], FMT)
    b1 = bf(np.random.standard_normal(F) * 0.3)
    g1 = bf(1.0 + 0.1 * np.random.standard_normal(F))
    be1 = bf(np.random.standard_normal(F) * 0.2)
    W2_words, W2_scales = pack_weight(np.random.standard_normal((F, MEM)) / np.sqrt(F), FMT)
    b2 = bf(np.random.standard_normal(MEM) * 0.2)
    return {"x": x,
            "h": h,
            "W1_words": W1_words,
            "W1_scales": W1_scales,
            "b1": b1,
            "g1": g1,
            "be1": be1,
            "W2_words": W2_words,
            "W2_scales": W2_scales,
            "b2": b2}


def reference(x, h, W1_words, W1_scales, b1, g1, be1, W2_words, W2_scales, b2):
    combined = np.concatenate([f64(h), f64(x)], axis=-1)
    u = (mxq(combined, 1, "e4m3") @ unpack_weight(W1_words, W1_scales, FMT)) + f64(b1)
    t = gelu_erf(layernorm(u, f64(g1), f64(be1)))
    return np.tanh((mxq(t, 1, "e4m3") @ unpack_weight(W2_words, W2_scales, FMT)) + f64(b2))

@@ -1,0 +1,217 @@
+from contextlib import ExitStack
+
+import concourse.mybir as mybir
+from concourse.masks import make_identity
+
+F32 = mybir.dt.float32
+BF16 = mybir.dt.bfloat16
+I32 = mybir.dt.int32
+U32 = mybir.dt.uint32
+U8 = mybir.dt.uint8
+FP8X4 = mybir.dt.float8_e4m3fn_x4
+ACT = mybir.ActivationFunctionType
+ALU = mybir.AluOpType
+
+P = 128
+PACK = 4
+ROWS = 8192
+HALF = 256
+FEAT = 512
+OUT = 256
+TILES = ROWS // P
+GROUP = 4
+PAIR = 2
+LN_EPS = 1e-5
+
+FLOPS = 2 * ROWS * FEAT * FEAT + 2 * ROWS * FEAT * OUT
+
+
+def load_weight(nc, pool, words_dram, scales_dram, width, name):
+    words = pool.tile([P, width], U32, name=name + "_words", align_bytes=64)
+    plane = pool.tile([P, width], U8, name=name + "_plane", align_bytes=64)
+    nc.vector.memset(plane[:].bitcast(I32), 0)
+    nc.sync.dma_start(out=words[:].bitcast(I32), in_=words_dram[0].rearrange("p n t -> p (n t)").bitcast(I32))
+    for quadrant in range(4):
+        nc.sync.dma_start(
+            out=plane[32 * quadrant : 32 * quadrant + 4, :].bitcast(I32),
+            in_=scales_dram[0, 4 * quadrant : 4 * quadrant + 4, :].bitcast(I32),
+        )
+    return words, plane
+
+
+def tile_liquidmemorycell_pa_t_kernel(
+    tc, x, h, W1_words, W1_scales, b1, g1, be1, W2_words, W2_scales, b2, out
+):
+    nc = tc.nc
+    x_rows = x.rearrange("(p j) k -> p j k", j=TILES)
+    h_rows = h.rearrange("(p j) k -> p j k", j=TILES)
+    out_rows = out.rearrange("(p j) n -> p j n", j=TILES)
+
+    with ExitStack() as stack:
+        const = stack.enter_context(tc.tile_pool(name="const", bufs=1))
+        loads = stack.enter_context(tc.tile_pool(name="loads", bufs=4))
+        work = stack.enter_context(tc.tile_pool(name="work", bufs=3))
+        stats = stack.enter_context(tc.tile_pool(name="stats", bufs=4))
+        ps_ct = stack.enter_context(tc.psum_pool(name="ps_ct", bufs=1))
+        ps_z = stack.enter_context(tc.psum_pool(name="ps_z", bufs=2))
+        ps_yt = stack.enter_context(tc.psum_pool(name="ps_yt", bufs=4))
+        ps_o = stack.enter_context(tc.psum_pool(name="ps_o", bufs=1))
+
+        warm = const.tile([P, 1], F32, name="warm")
+        nc.vector.memset(warm[:], 0.0)
+        nc.scalar.activation(out=warm[:], in_=warm[:], func=ACT.Gelu)
+
+        w1_words, w1_plane = load_weight(nc, const, W1_words, W1_scales, FEAT, "w1")
+        w2_words, w2_plane = load_weight(nc, const, W2_words, W2_scales, OUT, "w2")
+
+        ident = const.tile([P, P], F32, name="ident")
+        make_identity(nc, ident[:])
+
+        b1_raw = const.tile([P, FEAT], BF16, name="b1_raw")
+        nc.sync.dma_start(out=b1_raw[:], in_=b1.partition_broadcast(P))
+        b1_tq = const.tile([P, PACK, P], F32, name="b1_tq")
+        nc.vector.tensor_copy(out=b1_tq[:], in_=b1_raw[:].rearrange("p (q t) -> p t q", t=PACK))
+        b2_raw = const.tile([P, OUT], BF16, name="b2_raw")
+        nc.sync.dma_start(out=b2_raw[:], in_=b2.partition_broadcast(P))
+        b2_all = const.tile([P, OUT], F32, name="b2_all")
+        nc.vector.tensor_copy(out=b2_all[:], in_=b2_raw[:])
+        g1_raw = const.tile([P, PACK], BF16, name="g1_raw")
+        nc.sync.dma_start(out=g1_raw[:], in_=g1.rearrange("(q t) -> q t", t=PACK))
+        g1_qt = const.tile([P, PACK], F32, name="g1_qt")
+        nc.vector.tensor_copy(out=g1_qt[:], in_=g1_raw[:])
+        be1_raw = const.tile([P, PACK], BF16, name="be1_raw")
+        nc.sync.dma_start(out=be1_raw[:], in_=be1.rearrange("(q t) -> q t", t=PACK))
+        be1_qt = const.tile([P, PACK], F32, name="be1_qt")
+        nc.vector.tensor_copy(out=be1_qt[:], in_=be1_raw[:])
+        neg_half = const.tile([P, GROUP], F32, name="neg_half")
+        nc.vector.memset(neg_half[:], -0.5)
+
+        for g in range(TILES // GROUP):
+            tiles = slice(g * GROUP, (g + 1) * GROUP)
+
+            c_sb = loads.tile([P, GROUP, FEAT], BF16, name="c_sb")
+            nc.sync.dma_start(out=c_sb[:, :, 0:HALF], in_=h_rows[:, tiles, :])
+            nc.sync.dma_start(out=c_sb[:, :, HALF:FEAT], in_=x_rows[:, tiles, :])
+
+            c_pairs = c_sb[:].bitcast(F32)
+            c_grouped = work.tile([P, GROUP, P, PACK], BF16, name="c_grouped", align_bytes=64)
+            for half in range(GROUP // PAIR):
+                ct_ps = ps_ct.tile([P, PAIR, 2, P], F32, name="ct_ps")
+                for i in range(PAIR):
+                    for u in range(2):
+                        nc.tensor.transpose(
+                            ct_ps[:, i, u, :], c_pairs[:, half * PAIR + i, u : FEAT // 2 : 2], ident[:]
+                        )
+                nc.scalar.copy(
+                    out=c_grouped[:].bitcast(F32)[:, half * PAIR : (half + 1) * PAIR],
+                    in_=ct_ps[:].rearrange("p i u r -> p i r u"),
+                )
+            c_codes = work.tile([P, GROUP * P], U32, name="c_codes", align_bytes=64)
+            c_scales = work.tile([P, GROUP * P], U8, name="c_scales", align_bytes=64)
+            nc.vector.quantize_mx(
+                out=c_codes[:].bitcast(FP8X4),
+                scales=c_scales[:],
+                in_=c_grouped[:].rearrange("p j r t -> p (j r t)"),
+            )
+
+            u_sb = work.tile([P, GROUP, PACK, P], F32, name="u_sb")
+            sum_u = stats.tile([P, GROUP], F32, name="sum_u")
+            for j in range(GROUP):
+                rows = slice(j * P, (j + 1) * P)
+                z_ps = ps_z.tile([P, FEAT], F32, name="z_ps")
+                nc.tensor.matmul_mx(
+                    out=z_ps[:],
+                    lhsT=c_codes[:, rows].bitcast(FP8X4),
+                    lhsT_scale=c_scales[:, rows],
+                    rhs=w1_words[:].bitcast(FP8X4),
+                    rhs_scale=w1_plane[:],
+                    start=True,
+                    stop=True,
+                )
+                nc.vector.scalar_tensor_tensor(
+                    out=u_sb[:, j],
+                    in0=z_ps[:].rearrange("p (q t) -> p t q", t=PACK),
+                    scalar=1.0,
+                    in1=b1_tq[:],
+                    op0=ALU.mult,
+                    op1=ALU.add,
+                    accum_out=sum_u[:, j : j + 1],
+                )
+
+            neg_mu = stats.tile([P, GROUP], F32, name="neg_mu")
+            nc.vector.tensor_scalar(
+                out=neg_mu[:], in0=sum_u[:], scalar1=-1.0 / FEAT, scalar2=None, op0=ALU.mult
+            )
+            sum_sq = stats.tile([P, GROUP], F32, name="sum_sq")
+            for j in range(GROUP):
+                squares = work.tile([P, PACK, P], BF16, name="squares")
+                nc.scalar.activation(
+                    out=squares[:],
+                    in_=u_sb[:, j],
+                    func=ACT.Square,
+                    bias=neg_mu[:, j : j + 1],
+                    scale=1.0,
+                    accum_out=sum_sq[:, j : j + 1],
+                )
+            var_eps = stats.tile([P, GROUP], F32, name="var_eps")
+            nc.gpsimd.tensor_scalar(
+                out=var_eps[:], in0=sum_sq[:], scalar1=1.0 / FEAT, scalar2=LN_EPS, op0=ALU.mult, op1=ALU.add
+            )
+            rstd = stats.tile([P, GROUP], F32, name="rstd")
+            nc.gpsimd.tensor_tensor(out=rstd[:], in0=var_eps[:], in1=neg_half[:], op=ALU.pow)
+
+            for j in range(GROUP):
+                nc.vector.tensor_scalar(
+                    out=u_sb[:, j],
+                    in0=u_sb[:, j],
+                    scalar1=neg_mu[:, j : j + 1],
+                    scalar2=rstd[:, j : j + 1],
+                    op0=ALU.add,
+                    op1=ALU.mult,
+                )
+
+            t_planes = work.tile([P, PACK, GROUP * P], BF16, name="t_planes")
+            for t in range(PACK):
+                yt_ps = ps_yt.tile([P, GROUP * P], F32, name="yt_ps")
+                for j in range(GROUP):
+                    nc.tensor.transpose(yt_ps[:, j * P : (j + 1) * P], u_sb[:, j, t, :], ident[:])
+                nc.scalar.activation(
+                    out=t_planes[:, t, :],
+                    in_=yt_ps[:],
+                    func=ACT.Gelu,
+                    bias=be1_qt[:, t : t + 1],
+                    scale=g1_qt[:, t : t + 1],
+                )
+            t_grouped = work.tile([P, GROUP * P, PACK], BF16, name="t_grouped", align_bytes=64)
+            nc.vector.tensor_copy(out=t_grouped[:], in_=t_planes[:].rearrange("p t r -> p r t"))
+            t_codes = work.tile([P, GROUP * P], U32, name="t_codes", align_bytes=64)
+            t_scales = work.tile([P, GROUP * P], U8, name="t_scales", align_bytes=64)
+            nc.vector.quantize_mx(
+                out=t_codes[:].bitcast(FP8X4),
+                scales=t_scales[:],
+                in_=t_grouped[:].rearrange("p r t -> p (r t)"),
+            )
+
+            o_sb = work.tile([P, GROUP, OUT], F32, name="o_sb")
+            for half in range(GROUP // PAIR):
+                o_ps = ps_o.tile([P, PAIR, OUT], F32, name="o_ps")
+                for i in range(PAIR):
+                    j = half * PAIR + i
+                    rows = slice(j * P, (j + 1) * P)
+                    nc.tensor.matmul_mx(
+                        out=o_ps[:, i, :],
+                        lhsT=t_codes[:, rows].bitcast(FP8X4),
+                        lhsT_scale=t_scales[:, rows],
+                        rhs=w2_words[:].bitcast(FP8X4),
+                        rhs_scale=w2_plane[:],
+                        start=True,
+                        stop=True,
+                    )
+                nc.vector.tensor_tensor(
+                    out=o_sb[:, half * PAIR : (half + 1) * PAIR, :],
+                    in0=o_ps[:],
+                    in1=b2_all[:].unsqueeze(1).to_broadcast([P, PAIR, OUT]),
+                    op=ALU.add,
+                )
+            nc.scalar.activation(out=o_sb[:], in_=o_sb[:], func=ACT.Tanh)
+            nc.sync.dma_start(out=out_rows[:, tiles, :], in_=o_sb[:])

@@ -21,6 +21,7 @@ OUT = 256
 TILES = ROWS // P
 GROUP = 4
 PAIR = 2
+GROUPS = TILES // GROUP
 LN_EPS = 1e-5
 
 FLOPS = 2 * ROWS * FEAT * FEAT + 2 * ROWS * FEAT * OUT
@@ -48,170 +49,247 @@ def tile_liquidmemorycell_pa_t_kernel(
     out_rows = out.rearrange("(p j) n -> p j n", j=TILES)
 
     with ExitStack() as stack:
+        stack.enter_context(tc.manual_schedule())
         const = stack.enter_context(tc.tile_pool(name="const", bufs=1))
         loads = stack.enter_context(tc.tile_pool(name="loads", bufs=4))
-        work = stack.enter_context(tc.tile_pool(name="work", bufs=3))
-        stats = stack.enter_context(tc.tile_pool(name="stats", bufs=4))
-        ps_ct = stack.enter_context(tc.psum_pool(name="ps_ct", bufs=1))
-        ps_z = stack.enter_context(tc.psum_pool(name="ps_z", bufs=2))
-        ps_yt = stack.enter_context(tc.psum_pool(name="ps_yt", bufs=4))
-        ps_o = stack.enter_context(tc.psum_pool(name="ps_o", bufs=1))
+        long_lived = stack.enter_context(tc.tile_pool(name="long_lived", bufs=3))
+        work = stack.enter_context(tc.tile_pool(name="work", bufs=2))
+        psum = stack.enter_context(tc.psum_pool(name="psum", bufs=8))
 
-        warm = const.tile([P, 1], F32, name="warm")
-        nc.vector.memset(warm[:], 0.0)
-        nc.scalar.activation(out=warm[:], in_=warm[:], func=ACT.Gelu)
+        c_sb, c_grouped, c_codes, c_scales, ct_ps = {}, {}, {}, {}, {}
+        z_ps, u_sb, sum_u, neg_mu, rstd, yt_ps = {}, {}, {}, {}, {}, {}
+        t_planes, t_codes, t_scales, o_ps, o_sb = {}, {}, {}, {}, {}
 
-        w1_words, w1_plane = load_weight(nc, const, W1_words, W1_scales, FEAT, "w1")
-        w2_words, w2_plane = load_weight(nc, const, W2_words, W2_scales, OUT, "w2")
+        def in_range(g):
+            return 0 <= g < GROUPS
 
-        ident = const.tile([P, P], F32, name="ident")
-        make_identity(nc, ident[:])
-
-        b1_raw = const.tile([P, FEAT], BF16, name="b1_raw")
-        nc.sync.dma_start(out=b1_raw[:], in_=b1.partition_broadcast(P))
-        b1_tq = const.tile([P, PACK, P], F32, name="b1_tq")
-        nc.vector.tensor_copy(out=b1_tq[:], in_=b1_raw[:].rearrange("p (q t) -> p t q", t=PACK))
-        b2_raw = const.tile([P, OUT], BF16, name="b2_raw")
-        nc.sync.dma_start(out=b2_raw[:], in_=b2.partition_broadcast(P))
-        b2_all = const.tile([P, OUT], F32, name="b2_all")
-        nc.vector.tensor_copy(out=b2_all[:], in_=b2_raw[:])
-        g1_raw = const.tile([P, PACK], BF16, name="g1_raw")
-        nc.sync.dma_start(out=g1_raw[:], in_=g1.rearrange("(q t) -> q t", t=PACK))
-        g1_qt = const.tile([P, PACK], F32, name="g1_qt")
-        nc.vector.tensor_copy(out=g1_qt[:], in_=g1_raw[:])
-        be1_raw = const.tile([P, PACK], BF16, name="be1_raw")
-        nc.sync.dma_start(out=be1_raw[:], in_=be1.rearrange("(q t) -> q t", t=PACK))
-        be1_qt = const.tile([P, PACK], F32, name="be1_qt")
-        nc.vector.tensor_copy(out=be1_qt[:], in_=be1_raw[:])
-        neg_half = const.tile([P, GROUP], F32, name="neg_half")
-        nc.vector.memset(neg_half[:], -0.5)
-
-        for g in range(TILES // GROUP):
+        def load_c(g):
+            if not in_range(g):
+                return
             tiles = slice(g * GROUP, (g + 1) * GROUP)
+            c_sb[g] = loads.tile([P, GROUP, FEAT], BF16, name="c_sb")
+            nc.sync.dma_start(out=c_sb[g][:, :, 0:HALF], in_=h_rows[:, tiles, :])
+            nc.sync.dma_start(out=c_sb[g][:, :, HALF:FEAT], in_=x_rows[:, tiles, :])
 
-            c_sb = loads.tile([P, GROUP, FEAT], BF16, name="c_sb")
-            nc.sync.dma_start(out=c_sb[:, :, 0:HALF], in_=h_rows[:, tiles, :])
-            nc.sync.dma_start(out=c_sb[:, :, HALF:FEAT], in_=x_rows[:, tiles, :])
+        def transpose_c(g, half):
+            if not in_range(g):
+                return
+            c_pairs = c_sb[g][:].bitcast(F32)
+            bank = psum.tile([P, FEAT], F32, name="bank")
+            ct_ps[g, half] = bank[:].rearrange("p (i u r) -> p i u r", i=PAIR, u=2)
+            for i in range(PAIR):
+                for u in range(2):
+                    nc.tensor.transpose(
+                        ct_ps[g, half][:, i, u, :], c_pairs[:, half * PAIR + i, u : FEAT // 2 : 2], ident[:]
+                    )
 
-            c_pairs = c_sb[:].bitcast(F32)
-            c_grouped = work.tile([P, GROUP, P, PACK], BF16, name="c_grouped", align_bytes=64)
-            for half in range(GROUP // PAIR):
-                ct_ps = ps_ct.tile([P, PAIR, 2, P], F32, name="ct_ps")
-                for i in range(PAIR):
-                    for u in range(2):
-                        nc.tensor.transpose(
-                            ct_ps[:, i, u, :], c_pairs[:, half * PAIR + i, u : FEAT // 2 : 2], ident[:]
-                        )
-                nc.scalar.copy(
-                    out=c_grouped[:].bitcast(F32)[:, half * PAIR : (half + 1) * PAIR],
-                    in_=ct_ps[:].rearrange("p i u r -> p i r u"),
-                )
-            c_codes = work.tile([P, GROUP * P], U32, name="c_codes", align_bytes=64)
-            c_scales = work.tile([P, GROUP * P], U8, name="c_scales", align_bytes=64)
-            nc.vector.quantize_mx(
-                out=c_codes[:].bitcast(FP8X4),
-                scales=c_scales[:],
-                in_=c_grouped[:].rearrange("p j r t -> p (j r t)"),
+        def group_c(g, half):
+            if not in_range(g):
+                return
+            if half == 0:
+                c_grouped[g] = work.tile([P, GROUP, P, PACK], BF16, name="c_grouped", align_bytes=64)
+            nc.scalar.copy(
+                out=c_grouped[g][:].bitcast(F32)[:, half * PAIR : (half + 1) * PAIR],
+                in_=ct_ps[g, half].rearrange("p i u r -> p i r u"),
             )
 
-            u_sb = work.tile([P, GROUP, PACK, P], F32, name="u_sb")
-            sum_u = stats.tile([P, GROUP], F32, name="sum_u")
+        def quantise_c(g):
+            if not in_range(g):
+                return
+            c_codes[g] = work.tile([P, GROUP * P], U32, name="c_codes", align_bytes=64)
+            c_scales[g] = work.tile([P, GROUP * P], U8, name="c_scales", align_bytes=64)
+            nc.vector.quantize_mx(
+                out=c_codes[g][:].bitcast(FP8X4),
+                scales=c_scales[g][:],
+                in_=c_grouped[g][:].rearrange("p j r t -> p (j r t)"),
+            )
+
+        def first_matmul(g):
+            if not in_range(g):
+                return
             for j in range(GROUP):
                 rows = slice(j * P, (j + 1) * P)
-                z_ps = ps_z.tile([P, FEAT], F32, name="z_ps")
+                z_ps[g, j] = psum.tile([P, FEAT], F32, name="bank")
                 nc.tensor.matmul_mx(
-                    out=z_ps[:],
-                    lhsT=c_codes[:, rows].bitcast(FP8X4),
-                    lhsT_scale=c_scales[:, rows],
+                    out=z_ps[g, j][:],
+                    lhsT=c_codes[g][:, rows].bitcast(FP8X4),
+                    lhsT_scale=c_scales[g][:, rows],
                     rhs=w1_words[:].bitcast(FP8X4),
                     rhs_scale=w1_plane[:],
                     start=True,
                     stop=True,
                 )
+
+        def add_b1(g):
+            if not in_range(g):
+                return
+            u_sb[g] = long_lived.tile([P, GROUP, PACK, P], F32, name="u_sb")
+            sum_u[g] = long_lived.tile([P, GROUP], F32, name="sum_u")
+            for j in range(GROUP):
                 nc.vector.scalar_tensor_tensor(
-                    out=u_sb[:, j],
-                    in0=z_ps[:].rearrange("p (q t) -> p t q", t=PACK),
+                    out=u_sb[g][:, j],
+                    in0=z_ps[g, j][:].rearrange("p (q t) -> p t q", t=PACK),
                     scalar=1.0,
                     in1=b1_tq[:],
                     op0=ALU.mult,
                     op1=ALU.add,
-                    accum_out=sum_u[:, j : j + 1],
+                    accum_out=sum_u[g][:, j : j + 1],
                 )
-
-            neg_mu = stats.tile([P, GROUP], F32, name="neg_mu")
+            neg_mu[g] = long_lived.tile([P, GROUP], F32, name="neg_mu")
             nc.vector.tensor_scalar(
-                out=neg_mu[:], in0=sum_u[:], scalar1=-1.0 / FEAT, scalar2=None, op0=ALU.mult
+                out=neg_mu[g][:], in0=sum_u[g][:], scalar1=-1.0 / FEAT, scalar2=None, op0=ALU.mult
             )
-            sum_sq = stats.tile([P, GROUP], F32, name="sum_sq")
+
+        def spread(g):
+            if not in_range(g):
+                return
+            sum_sq = work.tile([P, GROUP], F32, name="sum_sq")
             for j in range(GROUP):
                 squares = work.tile([P, PACK, P], BF16, name="squares")
                 nc.scalar.activation(
                     out=squares[:],
-                    in_=u_sb[:, j],
+                    in_=u_sb[g][:, j],
                     func=ACT.Square,
-                    bias=neg_mu[:, j : j + 1],
+                    bias=neg_mu[g][:, j : j + 1],
                     scale=1.0,
                     accum_out=sum_sq[:, j : j + 1],
                 )
-            var_eps = stats.tile([P, GROUP], F32, name="var_eps")
+            var_eps = work.tile([P, GROUP], F32, name="var_eps")
             nc.gpsimd.tensor_scalar(
                 out=var_eps[:], in0=sum_sq[:], scalar1=1.0 / FEAT, scalar2=LN_EPS, op0=ALU.mult, op1=ALU.add
             )
-            rstd = stats.tile([P, GROUP], F32, name="rstd")
-            nc.gpsimd.tensor_tensor(out=rstd[:], in0=var_eps[:], in1=neg_half[:], op=ALU.pow)
+            rstd[g] = long_lived.tile([P, GROUP], F32, name="rstd")
+            nc.gpsimd.tensor_tensor(out=rstd[g][:], in0=var_eps[:], in1=neg_half[:], op=ALU.pow)
 
+        def normalise(g):
+            if not in_range(g):
+                return
             for j in range(GROUP):
                 nc.vector.tensor_scalar(
-                    out=u_sb[:, j],
-                    in0=u_sb[:, j],
-                    scalar1=neg_mu[:, j : j + 1],
-                    scalar2=rstd[:, j : j + 1],
+                    out=u_sb[g][:, j],
+                    in0=u_sb[g][:, j],
+                    scalar1=neg_mu[g][:, j : j + 1],
+                    scalar2=rstd[g][:, j : j + 1],
                     op0=ALU.add,
                     op1=ALU.mult,
                 )
 
-            t_planes = work.tile([P, PACK, GROUP * P], BF16, name="t_planes")
+        def transpose_y(g):
+            if not in_range(g):
+                return
             for t in range(PACK):
-                yt_ps = ps_yt.tile([P, GROUP * P], F32, name="yt_ps")
+                yt_ps[g, t] = psum.tile([P, GROUP * P], F32, name="bank")
                 for j in range(GROUP):
-                    nc.tensor.transpose(yt_ps[:, j * P : (j + 1) * P], u_sb[:, j, t, :], ident[:])
+                    nc.tensor.transpose(yt_ps[g, t][:, j * P : (j + 1) * P], u_sb[g][:, j, t, :], ident[:])
+
+        def gelu(g):
+            if not in_range(g):
+                return
+            t_planes[g] = long_lived.tile([P, PACK, GROUP * P], BF16, name="t_planes")
+            for t in range(PACK):
                 nc.scalar.activation(
-                    out=t_planes[:, t, :],
-                    in_=yt_ps[:],
+                    out=t_planes[g][:, t, :],
+                    in_=yt_ps[g, t][:],
                     func=ACT.Gelu,
                     bias=be1_qt[:, t : t + 1],
                     scale=g1_qt[:, t : t + 1],
                 )
+
+        def quantise_t(g):
+            if not in_range(g):
+                return
             t_grouped = work.tile([P, GROUP * P, PACK], BF16, name="t_grouped", align_bytes=64)
-            nc.vector.tensor_copy(out=t_grouped[:], in_=t_planes[:].rearrange("p t r -> p r t"))
-            t_codes = work.tile([P, GROUP * P], U32, name="t_codes", align_bytes=64)
-            t_scales = work.tile([P, GROUP * P], U8, name="t_scales", align_bytes=64)
+            nc.vector.tensor_copy(
+                out=t_grouped[:].rearrange("p (c i) t -> p c t i", i=4),
+                in_=t_planes[g][:].rearrange("p t (c i) -> p c t i", i=4),
+            )
+            t_codes[g] = work.tile([P, GROUP * P], U32, name="t_codes", align_bytes=64)
+            t_scales[g] = work.tile([P, GROUP * P], U8, name="t_scales", align_bytes=64)
             nc.vector.quantize_mx(
-                out=t_codes[:].bitcast(FP8X4),
-                scales=t_scales[:],
+                out=t_codes[g][:].bitcast(FP8X4),
+                scales=t_scales[g][:],
                 in_=t_grouped[:].rearrange("p r t -> p (r t)"),
             )
 
-            o_sb = work.tile([P, GROUP, OUT], F32, name="o_sb")
+        def second_matmul(g):
+            if not in_range(g):
+                return
             for half in range(GROUP // PAIR):
-                o_ps = ps_o.tile([P, PAIR, OUT], F32, name="o_ps")
+                bank = psum.tile([P, FEAT], F32, name="bank")
+                o_ps[g, half] = bank[:].rearrange("p (i n) -> p i n", i=PAIR)
                 for i in range(PAIR):
-                    j = half * PAIR + i
-                    rows = slice(j * P, (j + 1) * P)
+                    rows = slice((half * PAIR + i) * P, (half * PAIR + i + 1) * P)
                     nc.tensor.matmul_mx(
-                        out=o_ps[:, i, :],
-                        lhsT=t_codes[:, rows].bitcast(FP8X4),
-                        lhsT_scale=t_scales[:, rows],
+                        out=o_ps[g, half][:, i, :],
+                        lhsT=t_codes[g][:, rows].bitcast(FP8X4),
+                        lhsT_scale=t_scales[g][:, rows],
                         rhs=w2_words[:].bitcast(FP8X4),
                         rhs_scale=w2_plane[:],
                         start=True,
                         stop=True,
                     )
+
+        def add_b2(g):
+            if not in_range(g):
+                return
+            o_sb[g] = long_lived.tile([P, GROUP, OUT], F32, name="o_sb")
+            for half in range(GROUP // PAIR):
                 nc.vector.tensor_tensor(
-                    out=o_sb[:, half * PAIR : (half + 1) * PAIR, :],
-                    in0=o_ps[:],
+                    out=o_sb[g][:, half * PAIR : (half + 1) * PAIR, :],
+                    in0=o_ps[g, half],
                     in1=b2_all[:].unsqueeze(1).to_broadcast([P, PAIR, OUT]),
                     op=ALU.add,
                 )
-            nc.scalar.activation(out=o_sb[:], in_=o_sb[:], func=ACT.Tanh)
-            nc.sync.dma_start(out=out_rows[:, tiles, :], in_=o_sb[:])
+
+        def finish(g):
+            if not in_range(g):
+                return
+            nc.scalar.activation(out=o_sb[g][:], in_=o_sb[g][:], func=ACT.Tanh)
+            nc.sync.dma_start(out=out_rows[:, g * GROUP : (g + 1) * GROUP, :], in_=o_sb[g][:])
+
+        load_c(0)
+        warm = const.tile([P, 1], F32, name="warm")
+        nc.vector.memset(warm[:], 0.0)
+        nc.scalar.activation(out=warm[:], in_=warm[:], func=ACT.Gelu)
+        ident = const.tile([P, P], F32, name="ident")
+        make_identity(nc, ident[:])
+        w1_words, w1_plane = load_weight(nc, const, W1_words, W1_scales, FEAT, "w1")
+        load_c(1)
+        w2_words, w2_plane = load_weight(nc, const, W2_words, W2_scales, OUT, "w2")
+        neg_half = const.tile([P, GROUP], F32, name="neg_half")
+        nc.vector.memset(neg_half[:], -0.5)
+        b1_raw = const.tile([P, FEAT], BF16, name="b1_raw")
+        nc.scalar.dma_start(out=b1_raw[:], in_=b1.partition_broadcast(P))
+        b1_tq = const.tile([P, PACK, P], F32, name="b1_tq")
+        nc.vector.tensor_copy(out=b1_tq[:], in_=b1_raw[:].rearrange("p (q t) -> p t q", t=PACK))
+        g1_raw = const.tile([P, PACK], BF16, name="g1_raw")
+        nc.scalar.dma_start(out=g1_raw[:], in_=g1.rearrange("(q t) -> q t", t=PACK))
+        g1_qt = const.tile([P, PACK], F32, name="g1_qt")
+        nc.vector.tensor_copy(out=g1_qt[:], in_=g1_raw[:])
+        be1_raw = const.tile([P, PACK], BF16, name="be1_raw")
+        nc.scalar.dma_start(out=be1_raw[:], in_=be1.rearrange("(q t) -> q t", t=PACK))
+        be1_qt = const.tile([P, PACK], F32, name="be1_qt")
+        nc.vector.tensor_copy(out=be1_qt[:], in_=be1_raw[:])
+        b2_raw = const.tile([P, OUT], BF16, name="b2_raw")
+        nc.scalar.dma_start(out=b2_raw[:], in_=b2.partition_broadcast(P))
+        b2_all = const.tile([P, OUT], F32, name="b2_all")
+        nc.vector.tensor_copy(out=b2_all[:], in_=b2_raw[:])
+
+        load_c(2)
+        for i in range(GROUPS + 5):
+            load_c(i + 3)
+            gelu(i - 3)
+            add_b1(i - 1)
+            transpose_c(i, 0)
+            transpose_c(i, 1)
+            group_c(i, 0)
+            group_c(i, 1)
+            quantise_t(i - 4)
+            second_matmul(i - 4)
+            quantise_c(i)
+            first_matmul(i)
+            spread(i - 1)
+            finish(i - 5)
+            normalise(i - 2)
+            add_b2(i - 4)
+            transpose_y(i - 2)

@@ -88,7 +88,7 @@ def tile_liquidmemorycell_pa_t_kernel(
                 return
             if half == 0:
                 c_grouped[g] = work.tile([P, GROUP, P, PACK], BF16, name="c_grouped", align_bytes=64)
-            nc.scalar.copy(
+            nc.vector.tensor_copy(
                 out=c_grouped[g][:].bitcast(F32)[:, half * PAIR : (half + 1) * PAIR],
                 in_=ct_ps[g, half].rearrange("p i u r -> p i r u"),
             )
@@ -165,7 +165,7 @@ def tile_liquidmemorycell_pa_t_kernel(
             if not in_range(g):
                 return
             for j in range(GROUP):
-                nc.vector.tensor_scalar(
+                nc.gpsimd.tensor_scalar(
                     out=u_sb[g][:, j],
                     in0=u_sb[g][:, j],
                     scalar1=neg_mu[g][:, j : j + 1],
@@ -282,14 +282,14 @@ def tile_liquidmemorycell_pa_t_kernel(
             add_b1(i - 1)
             transpose_c(i, 0)
             transpose_c(i, 1)
-            group_c(i, 0)
-            group_c(i, 1)
             quantise_t(i - 4)
             second_matmul(i - 4)
+            group_c(i, 0)
+            group_c(i, 1)
             quantise_c(i)
             first_matmul(i)
             spread(i - 1)
+            normalise(i - 1)
             finish(i - 5)
-            normalise(i - 2)
             add_b2(i - 4)
             transpose_y(i - 2)

@@ -27,17 +27,20 @@ LN_EPS = 1e-5
 FLOPS = 2 * ROWS * FEAT * FEAT + 2 * ROWS * FEAT * OUT
 
 
-def load_weight(nc, pool, words_dram, scales_dram, width, name):
+def weight_tiles(nc, pool, width, name):
     words = pool.tile([P, width], U32, name=name + "_words", align_bytes=64)
     plane = pool.tile([P, width], U8, name=name + "_plane", align_bytes=64)
     nc.vector.memset(plane[:].bitcast(I32), 0)
+    return words, plane
+
+
+def load_weight(nc, words, plane, words_dram, scales_dram):
     nc.sync.dma_start(out=words[:].bitcast(I32), in_=words_dram[0].rearrange("p n t -> p (n t)").bitcast(I32))
     for quadrant in range(4):
         nc.sync.dma_start(
             out=plane[32 * quadrant : 32 * quadrant + 4, :].bitcast(I32),
             in_=scales_dram[0, 4 * quadrant : 4 * quadrant + 4, :].bitcast(I32),
         )
-    return words, plane
 
 
 def tile_liquidmemorycell_pa_t_kernel(
@@ -88,7 +91,7 @@ def tile_liquidmemorycell_pa_t_kernel(
                 return
             if half == 0:
                 c_grouped[g] = work.tile([P, GROUP, P, PACK], BF16, name="c_grouped", align_bytes=64)
-            nc.vector.tensor_copy(
+            nc.scalar.copy(
                 out=c_grouped[g][:].bitcast(F32)[:, half * PAIR : (half + 1) * PAIR],
                 in_=ct_ps[g, half].rearrange("p i u r -> p i r u"),
             )
@@ -165,7 +168,7 @@ def tile_liquidmemorycell_pa_t_kernel(
             if not in_range(g):
                 return
             for j in range(GROUP):
-                nc.gpsimd.tensor_scalar(
+                nc.vector.tensor_scalar(
                     out=u_sb[g][:, j],
                     in0=u_sb[g][:, j],
                     scalar1=neg_mu[g][:, j : j + 1],
@@ -247,49 +250,62 @@ def tile_liquidmemorycell_pa_t_kernel(
             nc.scalar.activation(out=o_sb[g][:], in_=o_sb[g][:], func=ACT.Tanh)
             nc.sync.dma_start(out=out_rows[:, g * GROUP : (g + 1) * GROUP, :], in_=o_sb[g][:])
 
-        load_c(0)
         warm = const.tile([P, 1], F32, name="warm")
         nc.vector.memset(warm[:], 0.0)
         nc.scalar.activation(out=warm[:], in_=warm[:], func=ACT.Gelu)
-        ident = const.tile([P, P], F32, name="ident")
-        make_identity(nc, ident[:])
-        w1_words, w1_plane = load_weight(nc, const, W1_words, W1_scales, FEAT, "w1")
-        load_c(1)
-        w2_words, w2_plane = load_weight(nc, const, W2_words, W2_scales, OUT, "w2")
+        w1_words, w1_plane = weight_tiles(nc, const, FEAT, "w1")
+        w2_words, w2_plane = weight_tiles(nc, const, OUT, "w2")
         neg_half = const.tile([P, GROUP], F32, name="neg_half")
         nc.vector.memset(neg_half[:], -0.5)
-        b1_raw = const.tile([P, FEAT], BF16, name="b1_raw")
-        nc.scalar.dma_start(out=b1_raw[:], in_=b1.partition_broadcast(P))
+        ident = const.tile([P, P], F32, name="ident")
+        make_identity(nc, ident[:])
+
+        load_c(0)
+        load_weight(nc, w1_words, w1_plane, W1_words, W1_scales)
+        load_c(1)
+        load_c(2)
+        load_weight(nc, w2_words, w2_plane, W2_words, W2_scales)
+
+        bias_rows = const.tile([P, FEAT + OUT], BF16, name="bias_rows")
+        nc.vector.memset(bias_rows[:], 0.0)
+        ones = const.tile([P, P], BF16, name="ones")
+        nc.vector.memset(ones[:], 1.0)
+        nc.scalar.dma_start(out=bias_rows[0:1, 0:FEAT], in_=b1.unsqueeze(0))
+        nc.scalar.dma_start(out=bias_rows[0:1, FEAT : FEAT + OUT], in_=b2.unsqueeze(0))
+        b1_ps = psum.tile([P, FEAT], F32, name="bank")
+        nc.tensor.matmul(out=b1_ps[:], lhsT=ones[:], rhs=bias_rows[:, 0:FEAT], start=True, stop=True)
         b1_tq = const.tile([P, PACK, P], F32, name="b1_tq")
-        nc.vector.tensor_copy(out=b1_tq[:], in_=b1_raw[:].rearrange("p (q t) -> p t q", t=PACK))
+        nc.vector.tensor_copy(out=b1_tq[:], in_=b1_ps[:].rearrange("p (q t) -> p t q", t=PACK))
+        b2_ps = psum.tile([P, FEAT], F32, name="bank")
+        nc.tensor.matmul(
+            out=b2_ps[:, 0:OUT], lhsT=ones[:], rhs=bias_rows[:, FEAT : FEAT + OUT], start=True, stop=True
+        )
+        b2_all = const.tile([P, OUT], F32, name="b2_all")
+        nc.vector.tensor_copy(out=b2_all[:], in_=b2_ps[:, 0:OUT])
+
         g1_raw = const.tile([P, PACK], BF16, name="g1_raw")
         nc.scalar.dma_start(out=g1_raw[:], in_=g1.rearrange("(q t) -> q t", t=PACK))
         g1_qt = const.tile([P, PACK], F32, name="g1_qt")
-        nc.vector.tensor_copy(out=g1_qt[:], in_=g1_raw[:])
+        nc.gpsimd.tensor_copy(out=g1_qt[:], in_=g1_raw[:])
         be1_raw = const.tile([P, PACK], BF16, name="be1_raw")
         nc.scalar.dma_start(out=be1_raw[:], in_=be1.rearrange("(q t) -> q t", t=PACK))
         be1_qt = const.tile([P, PACK], F32, name="be1_qt")
-        nc.vector.tensor_copy(out=be1_qt[:], in_=be1_raw[:])
-        b2_raw = const.tile([P, OUT], BF16, name="b2_raw")
-        nc.scalar.dma_start(out=b2_raw[:], in_=b2.partition_broadcast(P))
-        b2_all = const.tile([P, OUT], F32, name="b2_all")
-        nc.vector.tensor_copy(out=b2_all[:], in_=b2_raw[:])
+        nc.gpsimd.tensor_copy(out=be1_qt[:], in_=be1_raw[:])
 
-        load_c(2)
-        for i in range(GROUPS + 5):
+        for i in range(GROUPS + 7):
             load_c(i + 3)
-            gelu(i - 3)
-            add_b1(i - 1)
+            gelu(i - 4)
+            add_b1(i - 2)
             transpose_c(i, 0)
             transpose_c(i, 1)
-            quantise_t(i - 4)
-            second_matmul(i - 4)
             group_c(i, 0)
             group_c(i, 1)
-            quantise_c(i)
-            first_matmul(i)
-            spread(i - 1)
-            normalise(i - 1)
-            finish(i - 5)
-            add_b2(i - 4)
-            transpose_y(i - 2)
+            second_matmul(i - 6)
+            quantise_t(i - 5)
+            quantise_c(i - 1)
+            first_matmul(i - 1)
+            spread(i - 2)
+            finish(i - 7)
+            normalise(i - 3)
+            add_b2(i - 6)
+            transpose_y(i - 3)

@@ -61,7 +61,7 @@ def tile_liquidmemorycell_pa_t_kernel(
 
         c_sb, c_grouped, c_codes, c_scales, ct_ps = {}, {}, {}, {}, {}
         z_ps, u_sb, sum_u, neg_mu, rstd, yt_ps = {}, {}, {}, {}, {}, {}
-        t_planes, t_codes, t_scales, o_ps, o_sb = {}, {}, {}, {}, {}
+        t_planes, t_grouped, t_codes, t_scales, o_ps, o_sb = {}, {}, {}, {}, {}, {}
 
         def in_range(g):
             return 0 <= g < GROUPS
@@ -138,6 +138,10 @@ def tile_liquidmemorycell_pa_t_kernel(
                     op1=ALU.add,
                     accum_out=sum_u[g][:, j : j + 1],
                 )
+
+        def negate_mean(g):
+            if not in_range(g):
+                return
             neg_mu[g] = long_lived.tile([P, GROUP], F32, name="neg_mu")
             nc.vector.tensor_scalar(
                 out=neg_mu[g][:], in0=sum_u[g][:], scalar1=-1.0 / FEAT, scalar2=None, op0=ALU.mult
@@ -198,20 +202,24 @@ def tile_liquidmemorycell_pa_t_kernel(
                     scale=g1_qt[:, t : t + 1],
                 )
 
+        def interleave_t(g):
+            if not in_range(g):
+                return
+            t_grouped[g] = work.tile([P, GROUP * P, PACK], BF16, name="t_grouped", align_bytes=64)
+            nc.vector.tensor_copy(
+                out=t_grouped[g][:].rearrange("p (c i) t -> p c t i", i=4),
+                in_=t_planes[g][:].rearrange("p t (c i) -> p c t i", i=4),
+            )
+
         def quantise_t(g):
             if not in_range(g):
                 return
-            t_grouped = work.tile([P, GROUP * P, PACK], BF16, name="t_grouped", align_bytes=64)
-            nc.vector.tensor_copy(
-                out=t_grouped[:].rearrange("p (c i) t -> p c t i", i=4),
-                in_=t_planes[g][:].rearrange("p t (c i) -> p c t i", i=4),
-            )
             t_codes[g] = work.tile([P, GROUP * P], U32, name="t_codes", align_bytes=64)
             t_scales[g] = work.tile([P, GROUP * P], U8, name="t_scales", align_bytes=64)
             nc.vector.quantize_mx(
                 out=t_codes[g][:].bitcast(FP8X4),
                 scales=t_scales[g][:],
-                in_=t_grouped[:].rearrange("p r t -> p (r t)"),
+                in_=t_grouped[g][:].rearrange("p r t -> p (r t)"),
             )
 
         def second_matmul(g):
@@ -301,11 +309,13 @@ def tile_liquidmemorycell_pa_t_kernel(
             group_c(i, 0)
             group_c(i, 1)
             second_matmul(i - 6)
-            quantise_t(i - 5)
             quantise_c(i - 1)
+            negate_mean(i - 2)
+            interleave_t(i - 5)
             first_matmul(i - 1)
             spread(i - 2)
             finish(i - 7)
             normalise(i - 3)
+            quantise_t(i - 5)
             add_b2(i - 6)
             transpose_y(i - 3)

@@ -19,9 +19,13 @@ HALF = 256
 FEAT = 512
 OUT = 256
 TILES = ROWS // P
-GROUP = 4
 PAIR = 2
-GROUPS = TILES // GROUP
+GROUP = 4
+SIZES = [1, 1, 2] + [GROUP] * 14 + [2, 1, 1]
+STARTS = [sum(SIZES[:g]) for g in range(len(SIZES))]
+GROUPS = len(SIZES)
+GPSIMD_TILES = 2
+LOAD = 4
 LN_EPS = 1e-5
 
 FLOPS = 2 * ROWS * FEAT * FEAT + 2 * ROWS * FEAT * OUT
@@ -54,53 +58,57 @@ def tile_liquidmemorycell_pa_t_kernel(
     with ExitStack() as stack:
         stack.enter_context(tc.manual_schedule())
         const = stack.enter_context(tc.tile_pool(name="const", bufs=1))
-        loads = stack.enter_context(tc.tile_pool(name="loads", bufs=4))
-        long_lived = stack.enter_context(tc.tile_pool(name="long_lived", bufs=3))
+        loads = stack.enter_context(tc.tile_pool(name="loads", bufs=5))
+        stores = stack.enter_context(tc.tile_pool(name="stores", bufs=5))
+        long_lived = stack.enter_context(tc.tile_pool(name="long_lived", bufs=4))
         work = stack.enter_context(tc.tile_pool(name="work", bufs=2))
         psum = stack.enter_context(tc.psum_pool(name="psum", bufs=8))
 
         c_sb, c_grouped, c_codes, c_scales, ct_ps = {}, {}, {}, {}, {}
-        z_ps, u_sb, sum_u, neg_mu, rstd, yt_ps = {}, {}, {}, {}, {}, {}
+        z_ps, u_sb, sum_u, neg_mu, shift, rstd, yt_ps = {}, {}, {}, {}, {}, {}, {}
         t_planes, t_grouped, t_codes, t_scales, o_ps, o_sb = {}, {}, {}, {}, {}, {}
 
         def in_range(g):
             return 0 <= g < GROUPS
 
-        def load_c(g):
-            if not in_range(g):
+        def load_c(m):
+            if not 0 <= m < TILES // LOAD:
                 return
-            tiles = slice(g * GROUP, (g + 1) * GROUP)
-            c_sb[g] = loads.tile([P, GROUP, FEAT], BF16, name="c_sb")
-            nc.sync.dma_start(out=c_sb[g][:, :, 0:HALF], in_=h_rows[:, tiles, :])
-            nc.sync.dma_start(out=c_sb[g][:, :, HALF:FEAT], in_=x_rows[:, tiles, :])
+            tiles = slice(m * LOAD, (m + 1) * LOAD)
+            c_sb[m] = loads.tile([P, LOAD, FEAT], BF16, name="c_sb")
+            nc.sync.dma_start(out=c_sb[m][:, :, 0:HALF], in_=h_rows[:, tiles, :])
+            nc.sync.dma_start(out=c_sb[m][:, :, HALF:FEAT], in_=x_rows[:, tiles, :])
 
-        def transpose_c(g, half):
+        def transpose_c(g):
             if not in_range(g):
                 return
-            c_pairs = c_sb[g][:].bitcast(F32)
-            bank = psum.tile([P, FEAT], F32, name="bank")
-            ct_ps[g, half] = bank[:].rearrange("p (i u r) -> p i u r", i=PAIR, u=2)
-            for i in range(PAIR):
-                for u in range(2):
-                    nc.tensor.transpose(
-                        ct_ps[g, half][:, i, u, :], c_pairs[:, half * PAIR + i, u : FEAT // 2 : 2], ident[:]
-                    )
+            c_pairs = c_sb[STARTS[g] // LOAD][:].bitcast(F32)
+            at = STARTS[g] % LOAD
+            for first in range(0, SIZES[g], PAIR):
+                bank = psum.tile([P, FEAT], F32, name="bank")
+                ct_ps[g, first] = bank[:].rearrange("p (i u r) -> p i u r", i=PAIR, u=2)
+                for i in range(min(PAIR, SIZES[g] - first)):
+                    for u in range(2):
+                        nc.tensor.transpose(
+                            ct_ps[g, first][:, i, u, :], c_pairs[:, at + first + i, u : FEAT // 2 : 2], ident[:]
+                        )
 
-        def group_c(g, half):
+        def group_c(g):
             if not in_range(g):
                 return
-            if half == 0:
-                c_grouped[g] = work.tile([P, GROUP, P, PACK], BF16, name="c_grouped", align_bytes=64)
-            nc.scalar.copy(
-                out=c_grouped[g][:].bitcast(F32)[:, half * PAIR : (half + 1) * PAIR],
-                in_=ct_ps[g, half].rearrange("p i u r -> p i r u"),
-            )
+            c_grouped[g] = work.tile([P, SIZES[g], P, PACK], BF16, name="c_grouped", align_bytes=64)
+            for first in range(0, SIZES[g], PAIR):
+                tiles = min(PAIR, SIZES[g] - first)
+                nc.scalar.copy(
+                    out=c_grouped[g][:].bitcast(F32)[:, first : first + tiles],
+                    in_=ct_ps[g, first][:, 0:tiles].rearrange("p i u r -> p i r u"),
+                )
 
         def quantise_c(g):
             if not in_range(g):
                 return
-            c_codes[g] = work.tile([P, GROUP * P], U32, name="c_codes", align_bytes=64)
-            c_scales[g] = work.tile([P, GROUP * P], U8, name="c_scales", align_bytes=64)
+            c_codes[g] = work.tile([P, SIZES[g] * P], U32, name="c_codes", align_bytes=64)
+            c_scales[g] = work.tile([P, SIZES[g] * P], U8, name="c_scales", align_bytes=64)
             nc.vector.quantize_mx(
                 out=c_codes[g][:].bitcast(FP8X4),
                 scales=c_scales[g][:],
@@ -110,7 +118,7 @@ def tile_liquidmemorycell_pa_t_kernel(
         def first_matmul(g):
             if not in_range(g):
                 return
-            for j in range(GROUP):
+            for j in range(SIZES[g]):
                 rows = slice(j * P, (j + 1) * P)
                 z_ps[g, j] = psum.tile([P, FEAT], F32, name="bank")
                 nc.tensor.matmul_mx(
@@ -126,9 +134,9 @@ def tile_liquidmemorycell_pa_t_kernel(
         def add_b1(g):
             if not in_range(g):
                 return
-            u_sb[g] = long_lived.tile([P, GROUP, PACK, P], F32, name="u_sb")
-            sum_u[g] = long_lived.tile([P, GROUP], F32, name="sum_u")
-            for j in range(GROUP):
+            u_sb[g] = long_lived.tile([P, SIZES[g], PACK, P], F32, name="u_sb")
+            sum_u[g] = long_lived.tile([P, SIZES[g]], F32, name="sum_u")
+            for j in range(SIZES[g]):
                 nc.vector.scalar_tensor_tensor(
                     out=u_sb[g][:, j],
                     in0=z_ps[g, j][:].rearrange("p (q t) -> p t q", t=PACK),
@@ -142,16 +150,24 @@ def tile_liquidmemorycell_pa_t_kernel(
         def negate_mean(g):
             if not in_range(g):
                 return
-            neg_mu[g] = long_lived.tile([P, GROUP], F32, name="neg_mu")
+            neg_mu[g] = long_lived.tile([P, SIZES[g]], F32, name="neg_mu")
             nc.vector.tensor_scalar(
                 out=neg_mu[g][:], in0=sum_u[g][:], scalar1=-1.0 / FEAT, scalar2=None, op0=ALU.mult
+            )
+
+        def release(g):
+            if not in_range(g) or SIZES[g] < GROUP:
+                return
+            shift[g] = long_lived.tile([P, SIZES[g]], F32, name="shift")
+            nc.vector.tensor_scalar(
+                out=shift[g][:], in0=sum_u[g][:], scalar1=-1.0 / FEAT, scalar2=None, op0=ALU.mult
             )
 
         def spread(g):
             if not in_range(g):
                 return
-            sum_sq = work.tile([P, GROUP], F32, name="sum_sq")
-            for j in range(GROUP):
+            sum_sq = work.tile([P, SIZES[g]], F32, name="sum_sq")
+            for j in range(SIZES[g]):
                 squares = work.tile([P, PACK, P], BF16, name="squares")
                 nc.scalar.activation(
                     out=squares[:],
@@ -161,21 +177,26 @@ def tile_liquidmemorycell_pa_t_kernel(
                     scale=1.0,
                     accum_out=sum_sq[:, j : j + 1],
                 )
-            var_eps = work.tile([P, GROUP], F32, name="var_eps")
+            var_eps = work.tile([P, SIZES[g]], F32, name="var_eps")
             nc.gpsimd.tensor_scalar(
                 out=var_eps[:], in0=sum_sq[:], scalar1=1.0 / FEAT, scalar2=LN_EPS, op0=ALU.mult, op1=ALU.add
             )
-            rstd[g] = long_lived.tile([P, GROUP], F32, name="rstd")
-            nc.gpsimd.tensor_tensor(out=rstd[g][:], in0=var_eps[:], in1=neg_half[:], op=ALU.pow)
+            rstd[g] = long_lived.tile([P, SIZES[g]], F32, name="rstd")
+            nc.gpsimd.tensor_tensor(out=rstd[g][:], in0=var_eps[:], in1=neg_half[:, 0 : SIZES[g]], op=ALU.pow)
 
-        def normalise(g):
+        def normalise(g, engine):
             if not in_range(g):
                 return
-            for j in range(GROUP):
-                nc.vector.tensor_scalar(
+            on_gpsimd = GPSIMD_TILES if SIZES[g] == GROUP else 0
+            if engine == "gpsimd":
+                op, tiles, minus_mean = nc.gpsimd.tensor_scalar, range(on_gpsimd), shift.get(g)
+            else:
+                op, tiles, minus_mean = nc.vector.tensor_scalar, range(on_gpsimd, SIZES[g]), neg_mu[g]
+            for j in tiles:
+                op(
                     out=u_sb[g][:, j],
                     in0=u_sb[g][:, j],
-                    scalar1=neg_mu[g][:, j : j + 1],
+                    scalar1=minus_mean[:, j : j + 1],
                     scalar2=rstd[g][:, j : j + 1],
                     op0=ALU.add,
                     op1=ALU.mult,
@@ -184,19 +205,23 @@ def tile_liquidmemorycell_pa_t_kernel(
         def transpose_y(g):
             if not in_range(g):
                 return
+            rows = SIZES[g] * P
             for t in range(PACK):
-                yt_ps[g, t] = psum.tile([P, GROUP * P], F32, name="bank")
-                for j in range(GROUP):
+                at = t * rows % FEAT
+                if at == 0:
+                    bank = psum.tile([P, FEAT], F32, name="bank")
+                yt_ps[g, t] = bank[:, at : at + rows]
+                for j in range(SIZES[g]):
                     nc.tensor.transpose(yt_ps[g, t][:, j * P : (j + 1) * P], u_sb[g][:, j, t, :], ident[:])
 
         def gelu(g):
             if not in_range(g):
                 return
-            t_planes[g] = long_lived.tile([P, PACK, GROUP * P], BF16, name="t_planes")
+            t_planes[g] = long_lived.tile([P, PACK, SIZES[g] * P], BF16, name="t_planes")
             for t in range(PACK):
                 nc.scalar.activation(
                     out=t_planes[g][:, t, :],
-                    in_=yt_ps[g, t][:],
+                    in_=yt_ps[g, t],
                     func=ACT.Gelu,
                     bias=be1_qt[:, t : t + 1],
                     scale=g1_qt[:, t : t + 1],
@@ -205,7 +230,7 @@ def tile_liquidmemorycell_pa_t_kernel(
         def interleave_t(g):
             if not in_range(g):
                 return
-            t_grouped[g] = work.tile([P, GROUP * P, PACK], BF16, name="t_grouped", align_bytes=64)
+            t_grouped[g] = work.tile([P, SIZES[g] * P, PACK], BF16, name="t_grouped", align_bytes=64)
             nc.vector.tensor_copy(
                 out=t_grouped[g][:].rearrange("p (c i) t -> p c t i", i=4),
                 in_=t_planes[g][:].rearrange("p t (c i) -> p c t i", i=4),
@@ -214,8 +239,8 @@ def tile_liquidmemorycell_pa_t_kernel(
         def quantise_t(g):
             if not in_range(g):
                 return
-            t_codes[g] = work.tile([P, GROUP * P], U32, name="t_codes", align_bytes=64)
-            t_scales[g] = work.tile([P, GROUP * P], U8, name="t_scales", align_bytes=64)
+            t_codes[g] = work.tile([P, SIZES[g] * P], U32, name="t_codes", align_bytes=64)
+            t_scales[g] = work.tile([P, SIZES[g] * P], U8, name="t_scales", align_bytes=64)
             nc.vector.quantize_mx(
                 out=t_codes[g][:].bitcast(FP8X4),
                 scales=t_scales[g][:],
@@ -225,13 +250,13 @@ def tile_liquidmemorycell_pa_t_kernel(
         def second_matmul(g):
             if not in_range(g):
                 return
-            for half in range(GROUP // PAIR):
+            for first in range(0, SIZES[g], PAIR):
                 bank = psum.tile([P, FEAT], F32, name="bank")
-                o_ps[g, half] = bank[:].rearrange("p (i n) -> p i n", i=PAIR)
-                for i in range(PAIR):
-                    rows = slice((half * PAIR + i) * P, (half * PAIR + i + 1) * P)
+                o_ps[g, first] = bank[:].rearrange("p (i n) -> p i n", i=PAIR)
+                for i in range(min(PAIR, SIZES[g] - first)):
+                    rows = slice((first + i) * P, (first + i + 1) * P)
                     nc.tensor.matmul_mx(
-                        out=o_ps[g, half][:, i, :],
+                        out=o_ps[g, first][:, i, :],
                         lhsT=t_codes[g][:, rows].bitcast(FP8X4),
                         lhsT_scale=t_scales[g][:, rows],
                         rhs=w2_words[:].bitcast(FP8X4),
@@ -243,12 +268,13 @@ def tile_liquidmemorycell_pa_t_kernel(
         def add_b2(g):
             if not in_range(g):
                 return
-            o_sb[g] = long_lived.tile([P, GROUP, OUT], F32, name="o_sb")
-            for half in range(GROUP // PAIR):
+            o_sb[g] = stores.tile([P, SIZES[g], OUT], F32, name="o_sb")
+            for first in range(0, SIZES[g], PAIR):
+                tiles = min(PAIR, SIZES[g] - first)
                 nc.vector.tensor_tensor(
-                    out=o_sb[g][:, half * PAIR : (half + 1) * PAIR, :],
-                    in0=o_ps[g, half],
-                    in1=b2_all[:].unsqueeze(1).to_broadcast([P, PAIR, OUT]),
+                    out=o_sb[g][:, first : first + tiles, :],
+                    in0=o_ps[g, first][:, 0:tiles],
+                    in1=b2_all[:].unsqueeze(1).to_broadcast([P, tiles, OUT]),
                     op=ALU.add,
                 )
 
@@ -256,30 +282,36 @@ def tile_liquidmemorycell_pa_t_kernel(
             if not in_range(g):
                 return
             nc.scalar.activation(out=o_sb[g][:], in_=o_sb[g][:], func=ACT.Tanh)
-            nc.sync.dma_start(out=out_rows[:, g * GROUP : (g + 1) * GROUP, :], in_=o_sb[g][:])
+            nc.sync.dma_start(out=out_rows[:, STARTS[g] : STARTS[g] + SIZES[g], :], in_=o_sb[g][:])
 
         warm = const.tile([P, 1], F32, name="warm")
         nc.vector.memset(warm[:], 0.0)
         nc.scalar.activation(out=warm[:], in_=warm[:], func=ACT.Gelu)
+        ident = const.tile([P, P], F32, name="ident")
+        make_identity(nc, ident[:])
         w1_words, w1_plane = weight_tiles(nc, const, FEAT, "w1")
+        bias_rows = const.tile([P, FEAT + OUT], BF16, name="bias_rows")
+        nc.vector.memset(bias_rows[:], 0.0)
+        nc.scalar.dma_start(out=bias_rows[0:1, 0:FEAT], in_=b1.unsqueeze(0))
+        nc.scalar.dma_start(out=bias_rows[0:1, FEAT : FEAT + OUT], in_=b2.unsqueeze(0))
+        g1_raw = const.tile([P, PACK], BF16, name="g1_raw")
+        nc.scalar.dma_start(out=g1_raw[:], in_=g1.rearrange("(q t) -> q t", t=PACK))
+        be1_raw = const.tile([P, PACK], BF16, name="be1_raw")
+        nc.scalar.dma_start(out=be1_raw[:], in_=be1.rearrange("(q t) -> q t", t=PACK))
+        ones = const.tile([P, P], BF16, name="ones")
+        nc.vector.memset(ones[:], 1.0)
         w2_words, w2_plane = weight_tiles(nc, const, OUT, "w2")
         neg_half = const.tile([P, GROUP], F32, name="neg_half")
         nc.vector.memset(neg_half[:], -0.5)
-        ident = const.tile([P, P], F32, name="ident")
-        make_identity(nc, ident[:])
 
         load_c(0)
         load_weight(nc, w1_words, w1_plane, W1_words, W1_scales)
         load_c(1)
-        load_c(2)
         load_weight(nc, w2_words, w2_plane, W2_words, W2_scales)
 
-        bias_rows = const.tile([P, FEAT + OUT], BF16, name="bias_rows")
-        nc.vector.memset(bias_rows[:], 0.0)
-        ones = const.tile([P, P], BF16, name="ones")
-        nc.vector.memset(ones[:], 1.0)
-        nc.scalar.dma_start(out=bias_rows[0:1, 0:FEAT], in_=b1.unsqueeze(0))
-        nc.scalar.dma_start(out=bias_rows[0:1, FEAT : FEAT + OUT], in_=b2.unsqueeze(0))
+        transpose_c(0)
+        group_c(0)
+
         b1_ps = psum.tile([P, FEAT], F32, name="bank")
         nc.tensor.matmul(out=b1_ps[:], lhsT=ones[:], rhs=bias_rows[:, 0:FEAT], start=True, stop=True)
         b1_tq = const.tile([P, PACK, P], F32, name="b1_tq")
@@ -291,31 +323,27 @@ def tile_liquidmemorycell_pa_t_kernel(
         b2_all = const.tile([P, OUT], F32, name="b2_all")
         nc.vector.tensor_copy(out=b2_all[:], in_=b2_ps[:, 0:OUT])
 
-        g1_raw = const.tile([P, PACK], BF16, name="g1_raw")
-        nc.scalar.dma_start(out=g1_raw[:], in_=g1.rearrange("(q t) -> q t", t=PACK))
         g1_qt = const.tile([P, PACK], F32, name="g1_qt")
         nc.gpsimd.tensor_copy(out=g1_qt[:], in_=g1_raw[:])
-        be1_raw = const.tile([P, PACK], BF16, name="be1_raw")
-        nc.scalar.dma_start(out=be1_raw[:], in_=be1.rearrange("(q t) -> q t", t=PACK))
         be1_qt = const.tile([P, PACK], F32, name="be1_qt")
         nc.gpsimd.tensor_copy(out=be1_qt[:], in_=be1_raw[:])
 
         for i in range(GROUPS + 7):
-            load_c(i + 3)
+            load_c(i + 2)
             gelu(i - 4)
-            add_b1(i - 2)
-            transpose_c(i, 0)
-            transpose_c(i, 1)
-            group_c(i, 0)
-            group_c(i, 1)
-            second_matmul(i - 6)
-            quantise_c(i - 1)
-            negate_mean(i - 2)
-            interleave_t(i - 5)
-            first_matmul(i - 1)
-            spread(i - 2)
+            release(i - 3)
+            add_b1(i - 1)
+            normalise(i - 3, "gpsimd")
             finish(i - 7)
-            normalise(i - 3)
+            transpose_c(i + 1)
+            group_c(i + 1)
+            second_matmul(i - 6)
+            quantise_c(i)
+            negate_mean(i - 1)
+            interleave_t(i - 5)
+            first_matmul(i)
+            spread(i - 1)
+            normalise(i - 3, "vector")
             quantise_t(i - 5)
             add_b2(i - 6)
             transpose_y(i - 3)

@@ -21,7 +21,7 @@ OUT = 256
 TILES = ROWS // P
 PAIR = 2
 GROUP = 4
-SIZES = [1, 1, 2] + [GROUP] * 14 + [2, 1, 1]
+SIZES = [2, 2] + [GROUP] * 14 + [2, 2]
 STARTS = [sum(SIZES[:g]) for g in range(len(SIZES))]
 GROUPS = len(SIZES)
 GPSIMD_TILES = 2
@@ -61,6 +61,7 @@ def tile_liquidmemorycell_pa_t_kernel(
         loads = stack.enter_context(tc.tile_pool(name="loads", bufs=5))
         stores = stack.enter_context(tc.tile_pool(name="stores", bufs=5))
         long_lived = stack.enter_context(tc.tile_pool(name="long_lived", bufs=4))
+        ahead = stack.enter_context(tc.tile_pool(name="ahead", bufs=3))
         work = stack.enter_context(tc.tile_pool(name="work", bufs=2))
         psum = stack.enter_context(tc.psum_pool(name="psum", bufs=8))
 
@@ -96,7 +97,7 @@ def tile_liquidmemorycell_pa_t_kernel(
         def group_c(g):
             if not in_range(g):
                 return
-            c_grouped[g] = work.tile([P, SIZES[g], P, PACK], BF16, name="c_grouped", align_bytes=64)
+            c_grouped[g] = ahead.tile([P, SIZES[g], P, PACK], BF16, name="c_grouped", align_bytes=64)
             for first in range(0, SIZES[g], PAIR):
                 tiles = min(PAIR, SIZES[g] - first)
                 nc.scalar.copy(
@@ -107,8 +108,8 @@ def tile_liquidmemorycell_pa_t_kernel(
         def quantise_c(g):
             if not in_range(g):
                 return
-            c_codes[g] = work.tile([P, SIZES[g] * P], U32, name="c_codes", align_bytes=64)
-            c_scales[g] = work.tile([P, SIZES[g] * P], U8, name="c_scales", align_bytes=64)
+            c_codes[g] = ahead.tile([P, SIZES[g] * P], U32, name="c_codes", align_bytes=64)
+            c_scales[g] = ahead.tile([P, SIZES[g] * P], U8, name="c_scales", align_bytes=64)
             nc.vector.quantize_mx(
                 out=c_codes[g][:].bitcast(FP8X4),
                 scales=c_scales[g][:],
@@ -293,11 +294,6 @@ def tile_liquidmemorycell_pa_t_kernel(
         bias_rows = const.tile([P, FEAT + OUT], BF16, name="bias_rows")
         nc.vector.memset(bias_rows[:], 0.0)
         nc.scalar.dma_start(out=bias_rows[0:1, 0:FEAT], in_=b1.unsqueeze(0))
-        nc.scalar.dma_start(out=bias_rows[0:1, FEAT : FEAT + OUT], in_=b2.unsqueeze(0))
-        g1_raw = const.tile([P, PACK], BF16, name="g1_raw")
-        nc.scalar.dma_start(out=g1_raw[:], in_=g1.rearrange("(q t) -> q t", t=PACK))
-        be1_raw = const.tile([P, PACK], BF16, name="be1_raw")
-        nc.scalar.dma_start(out=be1_raw[:], in_=be1.rearrange("(q t) -> q t", t=PACK))
         ones = const.tile([P, P], BF16, name="ones")
         nc.vector.memset(ones[:], 1.0)
         w2_words, w2_plane = weight_tiles(nc, const, OUT, "w2")
@@ -311,22 +307,33 @@ def tile_liquidmemorycell_pa_t_kernel(
 
         transpose_c(0)
         group_c(0)
+        quantise_c(0)
 
         b1_ps = psum.tile([P, FEAT], F32, name="bank")
         nc.tensor.matmul(out=b1_ps[:], lhsT=ones[:], rhs=bias_rows[:, 0:FEAT], start=True, stop=True)
         b1_tq = const.tile([P, PACK, P], F32, name="b1_tq")
         nc.vector.tensor_copy(out=b1_tq[:], in_=b1_ps[:].rearrange("p (q t) -> p t q", t=PACK))
-        b2_ps = psum.tile([P, FEAT], F32, name="bank")
-        nc.tensor.matmul(
-            out=b2_ps[:, 0:OUT], lhsT=ones[:], rhs=bias_rows[:, FEAT : FEAT + OUT], start=True, stop=True
-        )
-        b2_all = const.tile([P, OUT], F32, name="b2_all")
-        nc.vector.tensor_copy(out=b2_all[:], in_=b2_ps[:, 0:OUT])
+        transpose_c(1)
+        group_c(1)
+        first_matmul(0)
 
+        nc.scalar.dma_start(out=bias_rows[0:1, FEAT : FEAT + OUT], in_=b2.unsqueeze(0))
+        g1_raw = const.tile([P, PACK], BF16, name="g1_raw")
+        nc.scalar.dma_start(out=g1_raw[:], in_=g1.rearrange("(q t) -> q t", t=PACK))
+        be1_raw = const.tile([P, PACK], BF16, name="be1_raw")
+        nc.scalar.dma_start(out=be1_raw[:], in_=be1.rearrange("(q t) -> q t", t=PACK))
         g1_qt = const.tile([P, PACK], F32, name="g1_qt")
         nc.gpsimd.tensor_copy(out=g1_qt[:], in_=g1_raw[:])
         be1_qt = const.tile([P, PACK], F32, name="be1_qt")
         nc.gpsimd.tensor_copy(out=be1_qt[:], in_=be1_raw[:])
+        b2_all = const.tile([P, OUT], F32, name="b2_all")
+
+        def spread_b2():
+            b2_ps = psum.tile([P, FEAT], F32, name="bank")
+            nc.tensor.matmul(
+                out=b2_ps[:, 0:OUT], lhsT=ones[:], rhs=bias_rows[:, FEAT : FEAT + OUT], start=True, stop=True
+            )
+            nc.vector.tensor_copy(out=b2_all[:], in_=b2_ps[:, 0:OUT])
 
         for i in range(GROUPS + 7):
             load_c(i + 2)
@@ -335,13 +342,16 @@ def tile_liquidmemorycell_pa_t_kernel(
             add_b1(i - 1)
             normalise(i - 3, "gpsimd")
             finish(i - 7)
-            transpose_c(i + 1)
-            group_c(i + 1)
+            transpose_c(i + 2)
+            group_c(i + 2)
+            if i == 3:
+                spread_b2()
             second_matmul(i - 6)
-            quantise_c(i)
+            quantise_c(i + 1)
             negate_mean(i - 1)
             interleave_t(i - 5)
-            first_matmul(i)
+            if i > 0:
+                first_matmul(i)
             spread(i - 1)
             normalise(i - 3, "vector")
             quantise_t(i - 5)

@@ -66,7 +66,7 @@ def tile_liquidmemorycell_pa_t_kernel(
         psum = stack.enter_context(tc.psum_pool(name="psum", bufs=8))
 
         c_sb, c_grouped, c_codes, c_scales, ct_ps = {}, {}, {}, {}, {}
-        z_ps, u_sb, sum_u, neg_mu, shift, rstd, yt_ps = {}, {}, {}, {}, {}, {}, {}
+        z_ps, u_sb, sum_u, neg_mu, shift, sum_sq, rstd, yt_ps = {}, {}, {}, {}, {}, {}, {}, {}
         t_planes, t_grouped, t_codes, t_scales, o_ps, o_sb = {}, {}, {}, {}, {}, {}
 
         def in_range(g):
@@ -167,7 +167,7 @@ def tile_liquidmemorycell_pa_t_kernel(
         def spread(g):
             if not in_range(g):
                 return
-            sum_sq = work.tile([P, SIZES[g]], F32, name="sum_sq")
+            sum_sq[g] = work.tile([P, SIZES[g]], F32, name="sum_sq")
             for j in range(SIZES[g]):
                 squares = work.tile([P, PACK, P], BF16, name="squares")
                 nc.scalar.activation(
@@ -176,11 +176,15 @@ def tile_liquidmemorycell_pa_t_kernel(
                     func=ACT.Square,
                     bias=neg_mu[g][:, j : j + 1],
                     scale=1.0,
-                    accum_out=sum_sq[:, j : j + 1],
+                    accum_out=sum_sq[g][:, j : j + 1],
                 )
+
+        def inverse_std(g):
+            if not in_range(g):
+                return
             var_eps = work.tile([P, SIZES[g]], F32, name="var_eps")
             nc.gpsimd.tensor_scalar(
-                out=var_eps[:], in0=sum_sq[:], scalar1=1.0 / FEAT, scalar2=LN_EPS, op0=ALU.mult, op1=ALU.add
+                out=var_eps[:], in0=sum_sq[g][:], scalar1=1.0 / FEAT, scalar2=LN_EPS, op0=ALU.mult, op1=ALU.add
             )
             rstd[g] = long_lived.tile([P, SIZES[g]], F32, name="rstd")
             nc.gpsimd.tensor_tensor(out=rstd[g][:], in0=var_eps[:], in1=neg_half[:, 0 : SIZES[g]], op=ALU.pow)
@@ -338,9 +342,7 @@ def tile_liquidmemorycell_pa_t_kernel(
         for i in range(GROUPS + 7):
             load_c(i + 2)
             gelu(i - 4)
-            release(i - 3)
             add_b1(i - 1)
-            normalise(i - 3, "gpsimd")
             finish(i - 7)
             transpose_c(i + 2)
             group_c(i + 2)
@@ -355,5 +357,8 @@ def tile_liquidmemorycell_pa_t_kernel(
             spread(i - 1)
             normalise(i - 3, "vector")
             quantise_t(i - 5)
+            release(i - 2)
+            normalise(i - 2, "gpsimd")
+            inverse_std(i - 1)
             add_b2(i - 6)
             transpose_y(i - 3)

@@ -24,7 +24,7 @@ GROUP = 4
 SIZES = [2, 2] + [GROUP] * 14 + [2, 2]
 STARTS = [sum(SIZES[:g]) for g in range(len(SIZES))]
 GROUPS = len(SIZES)
-GPSIMD_TILES = 2
+GPSIMD_TILES = 3
 LOAD = 4
 LN_EPS = 1e-5
 
@@ -66,7 +66,7 @@ def tile_liquidmemorycell_pa_t_kernel(
         psum = stack.enter_context(tc.psum_pool(name="psum", bufs=8))
 
         c_sb, c_grouped, c_codes, c_scales, ct_ps = {}, {}, {}, {}, {}
-        z_ps, u_sb, sum_u, neg_mu, shift, sum_sq, rstd, yt_ps = {}, {}, {}, {}, {}, {}, {}, {}
+        z_ps, u_sb, sum_u, neg_mu, shift, sum_sq, var_eps, rstd, yt_ps = {}, {}, {}, {}, {}, {}, {}, {}, {}
         t_planes, t_grouped, t_codes, t_scales, o_ps, o_sb = {}, {}, {}, {}, {}, {}
 
         def in_range(g):
@@ -179,15 +179,19 @@ def tile_liquidmemorycell_pa_t_kernel(
                     accum_out=sum_sq[g][:, j : j + 1],
                 )
 
+        def variance(g):
+            if not in_range(g):
+                return
+            var_eps[g] = work.tile([P, SIZES[g]], F32, name="var_eps")
+            nc.scalar.activation(
+                out=var_eps[g][:], in_=sum_sq[g][:], func=ACT.Copy, scale=1.0 / FEAT, bias=LN_EPS
+            )
+
         def inverse_std(g):
             if not in_range(g):
                 return
-            var_eps = work.tile([P, SIZES[g]], F32, name="var_eps")
-            nc.gpsimd.tensor_scalar(
-                out=var_eps[:], in0=sum_sq[g][:], scalar1=1.0 / FEAT, scalar2=LN_EPS, op0=ALU.mult, op1=ALU.add
-            )
             rstd[g] = long_lived.tile([P, SIZES[g]], F32, name="rstd")
-            nc.gpsimd.tensor_tensor(out=rstd[g][:], in0=var_eps[:], in1=neg_half[:, 0 : SIZES[g]], op=ALU.pow)
+            nc.gpsimd.tensor_tensor(out=rstd[g][:], in0=var_eps[g][:], in1=neg_half[:, 0 : SIZES[g]], op=ALU.pow)
 
         def normalise(g, engine):
             if not in_range(g):
@@ -219,11 +223,12 @@ def tile_liquidmemorycell_pa_t_kernel(
                 for j in range(SIZES[g]):
                     nc.tensor.transpose(yt_ps[g, t][:, j * P : (j + 1) * P], u_sb[g][:, j, t, :], ident[:])
 
-        def gelu(g):
+        def gelu(g, planes):
             if not in_range(g):
                 return
-            t_planes[g] = long_lived.tile([P, PACK, SIZES[g] * P], BF16, name="t_planes")
-            for t in range(PACK):
+            if planes[0] == 0:
+                t_planes[g] = long_lived.tile([P, PACK, SIZES[g] * P], BF16, name="t_planes")
+            for t in planes:
                 nc.scalar.activation(
                     out=t_planes[g][:, t, :],
                     in_=yt_ps[g, t],
@@ -341,8 +346,11 @@ def tile_liquidmemorycell_pa_t_kernel(
 
         for i in range(GROUPS + 7):
             load_c(i + 2)
-            gelu(i - 4)
+            gelu(i - 4, range(0, 1))
+            variance(i - 2)
+            gelu(i - 4, range(1, PACK))
             add_b1(i - 1)
+            inverse_std(i - 2)
             finish(i - 7)
             transpose_c(i + 2)
             group_c(i + 2)
@@ -359,6 +367,5 @@ def tile_liquidmemorycell_pa_t_kernel(
             quantise_t(i - 5)
             release(i - 2)
             normalise(i - 2, "gpsimd")
-            inverse_std(i - 1)
             add_b2(i - 6)
             transpose_y(i - 3)

from contextlib import ExitStack

import concourse.mybir as mybir
from concourse.masks import make_identity

F32 = mybir.dt.float32
BF16 = mybir.dt.bfloat16
I32 = mybir.dt.int32
U32 = mybir.dt.uint32
U8 = mybir.dt.uint8
FP8X4 = mybir.dt.float8_e4m3fn_x4
ACT = mybir.ActivationFunctionType
ALU = mybir.AluOpType

P = 128
PACK = 4
ROWS = 8192
HALF = 256
FEAT = 512
OUT = 256
TILES = ROWS // P
PAIR = 2
GROUP = 4
SIZES = [2, 2] + [GROUP] * 14 + [2, 2]
STARTS = [sum(SIZES[:g]) for g in range(len(SIZES))]
GROUPS = len(SIZES)
GPSIMD_TILES = 3
LOAD = 4
LN_EPS = 1e-5

FLOPS = 2 * ROWS * FEAT * FEAT + 2 * ROWS * FEAT * OUT


def weight_tiles(nc, pool, width, name):
    words = pool.tile([P, width], U32, name=name + "_words", align_bytes=64)
    plane = pool.tile([P, width], U8, name=name + "_plane", align_bytes=64)
    nc.vector.memset(plane[:].bitcast(I32), 0)
    return words, plane


def load_weight(nc, words, plane, words_dram, scales_dram):
    nc.sync.dma_start(out=words[:].bitcast(I32), in_=words_dram[0].rearrange("p n t -> p (n t)").bitcast(I32))
    for quadrant in range(4):
        nc.sync.dma_start(
            out=plane[32 * quadrant : 32 * quadrant + 4, :].bitcast(I32),
            in_=scales_dram[0, 4 * quadrant : 4 * quadrant + 4, :].bitcast(I32),
        )


def tile_liquidmemorycell_pa_t_kernel(
    tc, x, h, W1_words, W1_scales, b1, g1, be1, W2_words, W2_scales, b2, out
):
    nc = tc.nc
    x_rows = x.rearrange("(p j) k -> p j k", j=TILES)
    h_rows = h.rearrange("(p j) k -> p j k", j=TILES)
    out_rows = out.rearrange("(p j) n -> p j n", j=TILES)

    with ExitStack() as stack:
        stack.enter_context(tc.manual_schedule())
        const = stack.enter_context(tc.tile_pool(name="const", bufs=1))
        loads = stack.enter_context(tc.tile_pool(name="loads", bufs=5))
        stores = stack.enter_context(tc.tile_pool(name="stores", bufs=5))
        long_lived = stack.enter_context(tc.tile_pool(name="long_lived", bufs=4))
        ahead = stack.enter_context(tc.tile_pool(name="ahead", bufs=3))
        work = stack.enter_context(tc.tile_pool(name="work", bufs=2))
        psum = stack.enter_context(tc.psum_pool(name="psum", bufs=8))

        c_sb, c_grouped, c_codes, c_scales, ct_ps = {}, {}, {}, {}, {}
        z_ps, u_sb, sum_u, neg_mu, shift, sum_sq, var_eps, rstd, yt_ps = {}, {}, {}, {}, {}, {}, {}, {}, {}
        t_planes, t_grouped, t_codes, t_scales, o_ps, o_sb = {}, {}, {}, {}, {}, {}

        def in_range(g):
            return 0 <= g < GROUPS

        def load_c(m):
            if not 0 <= m < TILES // LOAD:
                return
            tiles = slice(m * LOAD, (m + 1) * LOAD)
            c_sb[m] = loads.tile([P, LOAD, FEAT], BF16, name="c_sb")
            nc.sync.dma_start(out=c_sb[m][:, :, 0:HALF], in_=h_rows[:, tiles, :])
            nc.sync.dma_start(out=c_sb[m][:, :, HALF:FEAT], in_=x_rows[:, tiles, :])

        def transpose_c(g):
            if not in_range(g):
                return
            c_pairs = c_sb[STARTS[g] // LOAD][:].bitcast(F32)
            at = STARTS[g] % LOAD
            for first in range(0, SIZES[g], PAIR):
                bank = psum.tile([P, FEAT], F32, name="bank")
                ct_ps[g, first] = bank[:].rearrange("p (i u r) -> p i u r", i=PAIR, u=2)
                for i in range(min(PAIR, SIZES[g] - first)):
                    for u in range(2):
                        nc.tensor.transpose(
                            ct_ps[g, first][:, i, u, :], c_pairs[:, at + first + i, u : FEAT // 2 : 2], ident[:]
                        )

        def group_c(g):
            if not in_range(g):
                return
            c_grouped[g] = ahead.tile([P, SIZES[g], P, PACK], BF16, name="c_grouped", align_bytes=64)
            for first in range(0, SIZES[g], PAIR):
                tiles = min(PAIR, SIZES[g] - first)
                nc.scalar.copy(
                    out=c_grouped[g][:].bitcast(F32)[:, first : first + tiles],
                    in_=ct_ps[g, first][:, 0:tiles].rearrange("p i u r -> p i r u"),
                )

        def quantise_c(g):
            if not in_range(g):
                return
            c_codes[g] = ahead.tile([P, SIZES[g] * P], U32, name="c_codes", align_bytes=64)
            c_scales[g] = ahead.tile([P, SIZES[g] * P], U8, name="c_scales", align_bytes=64)
            nc.vector.quantize_mx(
                out=c_codes[g][:].bitcast(FP8X4),
                scales=c_scales[g][:],
                in_=c_grouped[g][:].rearrange("p j r t -> p (j r t)"),
            )

        def first_matmul(g):
            if not in_range(g):
                return
            for j in range(SIZES[g]):
                rows = slice(j * P, (j + 1) * P)
                z_ps[g, j] = psum.tile([P, FEAT], F32, name="bank")
                nc.tensor.matmul_mx(
                    out=z_ps[g, j][:],
                    lhsT=c_codes[g][:, rows].bitcast(FP8X4),
                    lhsT_scale=c_scales[g][:, rows],
                    rhs=w1_words[:].bitcast(FP8X4),
                    rhs_scale=w1_plane[:],
                    start=True,
                    stop=True,
                )

        def add_b1(g):
            if not in_range(g):
                return
            u_sb[g] = long_lived.tile([P, SIZES[g], PACK, P], F32, name="u_sb")
            sum_u[g] = long_lived.tile([P, SIZES[g]], F32, name="sum_u")
            for j in range(SIZES[g]):
                nc.vector.scalar_tensor_tensor(
                    out=u_sb[g][:, j],
                    in0=z_ps[g, j][:].rearrange("p (q t) -> p t q", t=PACK),
                    scalar=1.0,
                    in1=b1_tq[:],
                    op0=ALU.mult,
                    op1=ALU.add,
                    accum_out=sum_u[g][:, j : j + 1],
                )

        def negate_mean(g):
            if not in_range(g):
                return
            neg_mu[g] = long_lived.tile([P, SIZES[g]], F32, name="neg_mu")
            nc.vector.tensor_scalar(
                out=neg_mu[g][:], in0=sum_u[g][:], scalar1=-1.0 / FEAT, scalar2=None, op0=ALU.mult
            )

        def release(g):
            if not in_range(g) or SIZES[g] < GROUP:
                return
            shift[g] = long_lived.tile([P, SIZES[g]], F32, name="shift")
            nc.vector.tensor_scalar(
                out=shift[g][:], in0=sum_u[g][:], scalar1=-1.0 / FEAT, scalar2=None, op0=ALU.mult
            )

        def spread(g):
            if not in_range(g):
                return
            sum_sq[g] = work.tile([P, SIZES[g]], F32, name="sum_sq")
            for j in range(SIZES[g]):
                squares = work.tile([P, PACK, P], BF16, name="squares")
                nc.scalar.activation(
                    out=squares[:],
                    in_=u_sb[g][:, j],
                    func=ACT.Square,
                    bias=neg_mu[g][:, j : j + 1],
                    scale=1.0,
                    accum_out=sum_sq[g][:, j : j + 1],
                )

        def variance(g):
            if not in_range(g):
                return
            var_eps[g] = work.tile([P, SIZES[g]], F32, name="var_eps")
            nc.scalar.activation(
                out=var_eps[g][:], in_=sum_sq[g][:], func=ACT.Copy, scale=1.0 / FEAT, bias=LN_EPS
            )

        def inverse_std(g):
            if not in_range(g):
                return
            rstd[g] = long_lived.tile([P, SIZES[g]], F32, name="rstd")
            nc.gpsimd.tensor_tensor(out=rstd[g][:], in0=var_eps[g][:], in1=neg_half[:, 0 : SIZES[g]], op=ALU.pow)

        def normalise(g, engine):
            if not in_range(g):
                return
            on_gpsimd = GPSIMD_TILES if SIZES[g] == GROUP else 0
            if engine == "gpsimd":
                op, tiles, minus_mean = nc.gpsimd.tensor_scalar, range(on_gpsimd), shift.get(g)
            else:
                op, tiles, minus_mean = nc.vector.tensor_scalar, range(on_gpsimd, SIZES[g]), neg_mu[g]
            for j in tiles:
                op(
                    out=u_sb[g][:, j],
                    in0=u_sb[g][:, j],
                    scalar1=minus_mean[:, j : j + 1],
                    scalar2=rstd[g][:, j : j + 1],
                    op0=ALU.add,
                    op1=ALU.mult,
                )

        def transpose_y(g):
            if not in_range(g):
                return
            rows = SIZES[g] * P
            for t in range(PACK):
                at = t * rows % FEAT
                if at == 0:
                    bank = psum.tile([P, FEAT], F32, name="bank")
                yt_ps[g, t] = bank[:, at : at + rows]
                for j in range(SIZES[g]):
                    nc.tensor.transpose(yt_ps[g, t][:, j * P : (j + 1) * P], u_sb[g][:, j, t, :], ident[:])

        def gelu(g, planes):
            if not in_range(g):
                return
            if planes[0] == 0:
                t_planes[g] = long_lived.tile([P, PACK, SIZES[g] * P], BF16, name="t_planes")
            for t in planes:
                nc.scalar.activation(
                    out=t_planes[g][:, t, :],
                    in_=yt_ps[g, t],
                    func=ACT.Gelu,
                    bias=be1_qt[:, t : t + 1],
                    scale=g1_qt[:, t : t + 1],
                )

        def interleave_t(g):
            if not in_range(g):
                return
            t_grouped[g] = work.tile([P, SIZES[g] * P, PACK], BF16, name="t_grouped", align_bytes=64)
            nc.vector.tensor_copy(
                out=t_grouped[g][:].rearrange("p (c i) t -> p c t i", i=4),
                in_=t_planes[g][:].rearrange("p t (c i) -> p c t i", i=4),
            )

        def quantise_t(g):
            if not in_range(g):
                return
            t_codes[g] = work.tile([P, SIZES[g] * P], U32, name="t_codes", align_bytes=64)
            t_scales[g] = work.tile([P, SIZES[g] * P], U8, name="t_scales", align_bytes=64)
            nc.vector.quantize_mx(
                out=t_codes[g][:].bitcast(FP8X4),
                scales=t_scales[g][:],
                in_=t_grouped[g][:].rearrange("p r t -> p (r t)"),
            )

        def second_matmul(g):
            if not in_range(g):
                return
            for first in range(0, SIZES[g], PAIR):
                bank = psum.tile([P, FEAT], F32, name="bank")
                o_ps[g, first] = bank[:].rearrange("p (i n) -> p i n", i=PAIR)
                for i in range(min(PAIR, SIZES[g] - first)):
                    rows = slice((first + i) * P, (first + i + 1) * P)
                    nc.tensor.matmul_mx(
                        out=o_ps[g, first][:, i, :],
                        lhsT=t_codes[g][:, rows].bitcast(FP8X4),
                        lhsT_scale=t_scales[g][:, rows],
                        rhs=w2_words[:].bitcast(FP8X4),
                        rhs_scale=w2_plane[:],
                        start=True,
                        stop=True,
                    )

        def add_b2(g):
            if not in_range(g):
                return
            o_sb[g] = stores.tile([P, SIZES[g], OUT], F32, name="o_sb")
            for first in range(0, SIZES[g], PAIR):
                tiles = min(PAIR, SIZES[g] - first)
                nc.vector.tensor_tensor(
                    out=o_sb[g][:, first : first + tiles, :],
                    in0=o_ps[g, first][:, 0:tiles],
                    in1=b2_all[:].unsqueeze(1).to_broadcast([P, tiles, OUT]),
                    op=ALU.add,
                )

        def finish(g):
            if not in_range(g):
                return
            nc.scalar.activation(out=o_sb[g][:], in_=o_sb[g][:], func=ACT.Tanh)
            nc.sync.dma_start(out=out_rows[:, STARTS[g] : STARTS[g] + SIZES[g], :], in_=o_sb[g][:])

        warm = const.tile([P, 1], F32, name="warm")
        nc.vector.memset(warm[:], 0.0)
        nc.scalar.activation(out=warm[:], in_=warm[:], func=ACT.Gelu)
        ident = const.tile([P, P], F32, name="ident")
        make_identity(nc, ident[:])
        w1_words, w1_plane = weight_tiles(nc, const, FEAT, "w1")
        bias_rows = const.tile([P, FEAT + OUT], BF16, name="bias_rows")
        nc.vector.memset(bias_rows[:], 0.0)
        nc.scalar.dma_start(out=bias_rows[0:1, 0:FEAT], in_=b1.unsqueeze(0))
        ones = const.tile([P, P], BF16, name="ones")
        nc.vector.memset(ones[:], 1.0)
        w2_words, w2_plane = weight_tiles(nc, const, OUT, "w2")
        neg_half = const.tile([P, GROUP], F32, name="neg_half")
        nc.vector.memset(neg_half[:], -0.5)

        load_c(0)
        load_weight(nc, w1_words, w1_plane, W1_words, W1_scales)
        load_c(1)
        load_weight(nc, w2_words, w2_plane, W2_words, W2_scales)

        transpose_c(0)
        group_c(0)
        quantise_c(0)

        b1_ps = psum.tile([P, FEAT], F32, name="bank")
        nc.tensor.matmul(out=b1_ps[:], lhsT=ones[:], rhs=bias_rows[:, 0:FEAT], start=True, stop=True)
        b1_tq = const.tile([P, PACK, P], F32, name="b1_tq")
        nc.vector.tensor_copy(out=b1_tq[:], in_=b1_ps[:].rearrange("p (q t) -> p t q", t=PACK))
        transpose_c(1)
        group_c(1)
        first_matmul(0)

        nc.scalar.dma_start(out=bias_rows[0:1, FEAT : FEAT + OUT], in_=b2.unsqueeze(0))
        g1_raw = const.tile([P, PACK], BF16, name="g1_raw")
        nc.scalar.dma_start(out=g1_raw[:], in_=g1.rearrange("(q t) -> q t", t=PACK))
        be1_raw = const.tile([P, PACK], BF16, name="be1_raw")
        nc.scalar.dma_start(out=be1_raw[:], in_=be1.rearrange("(q t) -> q t", t=PACK))
        g1_qt = const.tile([P, PACK], F32, name="g1_qt")
        nc.gpsimd.tensor_copy(out=g1_qt[:], in_=g1_raw[:])
        be1_qt = const.tile([P, PACK], F32, name="be1_qt")
        nc.gpsimd.tensor_copy(out=be1_qt[:], in_=be1_raw[:])
        b2_all = const.tile([P, OUT], F32, name="b2_all")

        def spread_b2():
            b2_ps = psum.tile([P, FEAT], F32, name="bank")
            nc.tensor.matmul(
                out=b2_ps[:, 0:OUT], lhsT=ones[:], rhs=bias_rows[:, FEAT : FEAT + OUT], start=True, stop=True
            )
            nc.vector.tensor_copy(out=b2_all[:], in_=b2_ps[:, 0:OUT])

        for i in range(GROUPS + 7):
            load_c(i + 2)
            gelu(i - 4, range(0, 1))
            variance(i - 2)
            gelu(i - 4, range(1, PACK))
            add_b1(i - 1)
            inverse_std(i - 2)
            finish(i - 7)
            transpose_c(i + 2)
            group_c(i + 2)
            if i == 3:
                spread_b2()
            second_matmul(i - 6)
            quantise_c(i + 1)
            negate_mean(i - 1)
            interleave_t(i - 5)
            if i > 0:
                first_matmul(i)
            spread(i - 1)
            normalise(i - 3, "vector")
            quantise_t(i - 5)
            release(i - 2)
            normalise(i - 2, "gpsimd")
            add_b2(i - 6)
            transpose_y(i - 3)
